import numpy as np
import ml_dtypes


BF16 = ml_dtypes.bfloat16


def bf(x):
    return np.asarray(x, np.float32).astype(BF16)


def f64(x):
    return np.asarray(x).astype(np.float64)


E2M1 = np.array([0.0, 0.5, 1.0, 1.5, 2.0, 3.0, 4.0, 6.0, -0.0, -0.5, -1.0, -1.5, -2.0, -3.0, -4.0, -6.0])


def pack_weight(w, fmt):
    k, n = w.shape
    w = f64(bf(w)).reshape(k // 32, 32, n)
    amax = np.abs(w).max(1)
    if fmt == "e4m3":
        byte = np.frexp(amax)[1] - 1 + 127 - 7
    else:
        mant, ex = np.frexp(amax / 6.0)
        byte = np.where(mant > 0.5, ex, ex - 1) + 127
    byte = np.clip(np.where(amax > 0, byte, 1), 1, 254)
    scaled = (w * np.exp2(127.0 - byte)[:, None, :]).reshape(k, n).astype(np.float32)
    by_word = np.ascontiguousarray(scaled.reshape(k // 512, 128, 4, n).transpose(0, 1, 3, 2))
    if fmt == "e4m3":
        words = by_word.astype(ml_dtypes.float8_e4m3fn).view(np.uint8)
    else:
        c = by_word.astype(ml_dtypes.float4_e2m1fn).view(np.uint8) & 0xF
        words = c[..., 0::2] | (c[..., 1::2] << 4)
    return np.ascontiguousarray(words), np.ascontiguousarray(byte.astype(np.uint8).reshape(k // 512, 16, n))


def unpack_weight(words, scales, fmt):
    g, p, n, _ = words.shape
    if fmt == "e4m3":
        vals = np.ascontiguousarray(words).view(ml_dtypes.float8_e4m3fn).astype(np.float64)
    else:
        nib = np.empty((g, p, n, 4), np.uint8)
        nib[..., 0::2] = words & 0xF
        nib[..., 1::2] = words >> 4
        vals = E2M1[nib]
    vals = vals * np.repeat(np.exp2(scales.astype(np.float64) - 127.0), 8, axis=1)[..., None]
    return vals.transpose(0, 1, 3, 2).reshape(g * 512, n)

def pack4(w):
    words, scales = pack_weight(w, "e2m1")
    return words.reshape(words.shape[0], 128, -1), scales


def unpack4(words, scales):
    return unpack_weight(words.reshape(words.shape[0], 128, -1, 2), scales, "e2m1")


def kspread(k):
    return np.exp2(np.repeat(np.random.randint(-6, 7, k // 32), 32).astype(np.float64))


B, N1, N2, D, H, DH = 2, 512, 512, 4096, 8, 128
HD = H * DH
EPS = 1e-6
ROPE_THETA = 10000.0


def split_heads(qkv):
    b, n = qkv.shape[0], qkv.shape[1]
    r = qkv.reshape(b, n, 3, H, DH)
    return tuple(r[:, :, i].transpose(0, 2, 1, 3) for i in range(3))


def rmsnorm(x, gamma):
    inv = 1.0 / np.sqrt(np.mean(np.square(x), axis=-1, keepdims=True) + EPS)
    return x * inv * gamma


def rope(x):
    n, d = x.shape[-2], x.shape[-1]
    inv_freq = 1.0 / ROPE_THETA ** (np.arange(0, d, 2) / d)
    ang = np.arange(n)[:, None] * inv_freq
    cos, sin = np.cos(ang), np.sin(ang)
    x1, x2 = np.split(x, 2, axis=-1)
    return np.concatenate([x1 * cos - x2 * sin, x1 * sin + x2 * cos], axis=-1)


def setup_inputs():
    s1, s2 = kspread(D), kspread(D)
    x_1 = np.random.standard_normal((B, N1, D)) * s1
    x_2 = np.random.standard_normal((B, N2, D)) * s2
    x_1_words, x_1_scales = pack4(np.ascontiguousarray(x_1.reshape(B * N1, D).T))
    x_2_words, x_2_scales = pack4(np.ascontiguousarray(x_2.reshape(B * N2, D).T))
    words1, scales1 = pack4(np.random.standard_normal((D, 3 * HD)) / np.sqrt(D) / s1[:, None])
    b_qkv1 = bf(np.random.standard_normal(3 * HD) * 0.2)
    words2, scales2 = pack4(np.random.standard_normal((D, 3 * HD)) / np.sqrt(D) / s2[:, None])
    b_qkv2 = bf(np.random.standard_normal(3 * HD) * 0.2)
    return {"x_1_words": x_1_words,
            "x_1_scales": x_1_scales,
            "x_2_words": x_2_words,
            "x_2_scales": x_2_scales,
            "w_qkv1_words": words1,
            "w_qkv1_scales": scales1,
            "b_qkv1": b_qkv1,
            "w_qkv2_words": words2,
            "w_qkv2_scales": scales2,
            "b_qkv2": b_qkv2,
            "qg1": bf(1.2 + 0.1 * np.random.standard_normal(DH)),
            "kg1": bf(1.2 + 0.1 * np.random.standard_normal(DH)),
            "qg2": bf(1.2 + 0.1 * np.random.standard_normal(DH)),
            "kg2": bf(1.2 + 0.1 * np.random.standard_normal(DH))}


def reference(x_1_words, x_1_scales, x_2_words, x_2_scales, w_qkv1_words, w_qkv1_scales, b_qkv1, w_qkv2_words, w_qkv2_scales, b_qkv2, qg1, kg1, qg2, kg2):
    x_1 = unpack4(x_1_words, x_1_scales).T.reshape(B, N1, D)
    x_2 = unpack4(x_2_words, x_2_scales).T.reshape(B, N2, D)
    w1 = unpack4(w_qkv1_words, w_qkv1_scales)
    w2 = unpack4(w_qkv2_words, w_qkv2_scales)
    qs, ks, vs = [], [], []
    for x, w, b, qg, kg in ((x_1, w1, b_qkv1, qg1, kg1), (x_2, w2, b_qkv2, qg2, kg2)):
        qkv = (x @ w) + f64(b)
        q, k, v = split_heads(qkv)
        qs.append(rmsnorm(q, f64(qg)))
        ks.append(rmsnorm(k, f64(kg)))
        vs.append(v)
    q = np.concatenate(qs, axis=-2)
    k = np.concatenate(ks, axis=-2)
    v = np.concatenate(vs, axis=-2)
    return rope(q), rope(k), v

@@ -1,0 +1,275 @@
+import math
+from contextlib import ExitStack
+
+import concourse.mybir as mybir
+from concourse.masks import make_identity
+
+F32 = mybir.dt.float32
+BF16 = mybir.dt.bfloat16
+I32 = mybir.dt.int32
+U8 = mybir.dt.uint8
+FP4X4 = mybir.dt.float4_e2m1fn_x4
+ACT = mybir.ActivationFunctionType
+ALU = mybir.AluOpType
+
+P = 128
+B, N1, D, H, DH = 2, 512, 4096, 8, 128
+HALF = DH // 2
+PASSES = D // 512
+COLS = 512
+W_SLOTS = 8
+X_SLOTS = 3
+FLOPS = 2 * 2 * (B * N1) * D * (3 * H * DH)
+
+
+def tile_mmattn_pa_kernel(
+    tc, x_1_words, x_1_scales, x_2_words, x_2_scales,
+    w_qkv1_words, w_qkv1_scales, b_qkv1, w_qkv2_words, w_qkv2_scales, b_qkv2,
+    qg1, kg1, qg2, kg2, out_0, out_1, out_2,
+):
+    nc = tc.nc
+    x_words = (x_1_words, x_2_words)
+    x_scales = (x_1_scales, x_2_scales)
+    w_words = (w_qkv1_words, w_qkv2_words)
+    w_scales = (w_qkv1_scales, w_qkv2_scales)
+    outs = (out_0, out_1, out_2)
+
+    with ExitStack() as ctx:
+        keep = ctx.enter_context(tc.tile_pool(name="keep", bufs=1))
+        work = ctx.enter_context(tc.tile_pool(name="work", bufs=2))
+        psum = ctx.enter_context(tc.psum_pool(name="psum", bufs=1))
+        ctx.enter_context(tc.manual_schedule())
+
+        def block_tiles(kind, k):
+            codes = keep.tile([P, PASSES, 2 * COLS], U8, name=f"{kind}c{k}", align_bytes=256)
+            plane = keep.tile([P, PASSES, COLS], U8, name=f"{kind}s{k}", align_bytes=256)
+            return codes, plane
+
+        w_slot = [block_tiles("w", k) for k in range(W_SLOTS)]
+        x_slot = [block_tiles("x", k) for k in range(X_SLOTS)]
+
+        def zero_plane(engine, slot):
+            engine.memset(slot[1][:].rearrange("p g c -> p (g c)").bitcast(I32), 0)
+
+        def load_codes(slot, words, c, g0, g1):
+            nc.sync.dma_start(
+                out=slot[0][:, g0:g1, :].bitcast(I32),
+                in_=words[g0:g1, :, 2 * COLS * c : 2 * COLS * (c + 1)].rearrange("g p c -> p g c").bitcast(I32))
+
+        def load_scales(slot, scales, c):
+            for q in range(4):
+                nc.sync.dma_start(
+                    out=slot[1][32 * q : 32 * q + 4, :, :].bitcast(I32),
+                    in_=scales[:, 4 * q : 4 * q + 4, COLS * c : COLS * (c + 1)].rearrange("g r n -> r g n").bitcast(I32))
+
+        def load_block(slot, words, scales, c):
+            load_scales(slot, scales, c)
+            load_codes(slot, words, c, 0, 4)
+            load_codes(slot, words, c, 4, 8)
+
+        def bank(i, name="bank"):
+            return psum.tile([P, COLS], F32, name=f"{name}{i % 8}", tag=f"bank{i % 8}")
+
+        load_codes(w_slot[0], w_words[0], 0, 0, 1)
+        load_codes(x_slot[0], x_words[0], 0, 0, 1)
+
+        rows_b = keep.tile([P, COLS], BF16, name="rows_b")
+        rows_g = keep.tile([P, COLS], BF16, name="rows_g")
+        nc.vector.memset(rows_b[:].bitcast(I32), 0)
+        zero_plane(nc.gpsimd, w_slot[0])
+        zero_plane(nc.vector, x_slot[0])
+        nc.vector.memset(rows_g[:].bitcast(I32), 0)
+        zero_plane(nc.vector, w_slot[1])
+        zero_plane(nc.vector, w_slot[2])
+        zero_plane(nc.vector, w_slot[3])
+
+        nc.gpsimd.dma_start(out=rows_b[0:6, :], in_=b_qkv1.rearrange("(r c) -> r c", c=COLS))
+        ident = keep.tile([P, P], BF16, name="ident")
+        make_identity(nc, ident[:])
+        pos = keep.tile([P, 8], F32, name="pos")
+        nc.gpsimd.iota(pos[:], [[P, 8]], base=0, channel_multiplier=1, allow_small_or_imprecise_dtypes=True)
+        for j, gain in enumerate((qg1, kg1, qg2, kg2)):
+            nc.gpsimd.dma_start(out=rows_g[0:1, DH * j : DH * (j + 1)], in_=gain.rearrange("(r c) -> r c", r=1))
+        zero_plane(nc.gpsimd, w_slot[4])
+        zero_plane(nc.gpsimd, w_slot[5])
+        zero_plane(nc.gpsimd, x_slot[1])
+        zero_plane(nc.gpsimd, w_slot[6])
+        zero_plane(nc.gpsimd, w_slot[7])
+        zero_plane(nc.gpsimd, x_slot[2])
+
+        load_scales(x_slot[0], x_scales[0], 0)
+        load_scales(w_slot[0], w_scales[0], 0)
+        for g0, g1 in ((1, 2), (2, 4), (4, 8)):
+            load_codes(w_slot[0], w_words[0], 0, g0, g1)
+            load_codes(x_slot[0], x_words[0], 0, g0, g1)
+        for n in (1, 2, 3, 4):
+            load_block(w_slot[n], w_words[0], w_scales[0], n)
+        load_block(w_slot[5], w_words[0], w_scales[0], 5)
+        load_block(x_slot[1], x_words[0], x_scales[0], 1)
+
+        bias = [keep.tile([P, COLS], BF16, name=f"bias{n}") for n in range(6)]
+        for n in range(6):
+            ps = bank(n % 4)
+            nc.tensor.matmul(ps[:], lhsT=ident[:, n : n + 1].to_broadcast([P, P]), rhs=rows_b[:], start=True, stop=True)
+            nc.scalar.copy(out=bias[n][:], in_=ps[:])
+
+        turns = work.tile([P, 2, 8, HALF], F32, name="turns", tag="z", bufs=8)
+        nc.vector.tensor_scalar_mul(turns[:, 0, :, 0:1], pos[:].unsqueeze(2), 1.0 / (2.0 * math.pi))
+        w = 1
+        while w < HALF:
+            nc.vector.tensor_scalar_mul(turns[:, 0, :, w : 2 * w], turns[:, 0, :, 0:w], 10000.0 ** (-w / HALF))
+            w *= 2
+        nc.vector.tensor_scalar_add(turns[:, 1, :, :], turns[:, 0, :, :], 0.25)
+        whole_i = work.tile([P, 1024], I32, name="whole_i", tag="t1", bufs=4)
+        whole_f = work.tile([P, 1024], F32, name="whole_f", tag="t2", bufs=2)
+        frac = work.tile([P, 2, 8, HALF], F32, name="frac", tag="z", bufs=8)
+        flat_turns = turns[:].rearrange("p a t d -> p (a t d)")
+        nc.vector.tensor_copy(out=whole_i[:], in_=flat_turns)
+        nc.vector.tensor_copy(out=whole_f[:], in_=whole_i[:])
+        nc.vector.tensor_sub(frac[:].rearrange("p a t d -> p (a t d)"), flat_turns, whole_f[:])
+        cos = keep.tile([P, 8, HALF], F32, name="cos")
+        sin = keep.tile([P, 8, 2, HALF], F32, name="sin")
+        nc.scalar.activation(out=cos[:], in_=frac[:, 1, :, :], func=ACT.Sin, scale=2.0 * math.pi)
+        nc.scalar.activation(out=sin[:, :, 0, :], in_=frac[:, 0, :, :], func=ACT.Sin, scale=-2.0 * math.pi)
+        nc.scalar.activation(out=sin[:, :, 1, :], in_=frac[:, 0, :, :], func=ACT.Sin, scale=2.0 * math.pi)
+
+        gains = keep.tile([P, 4, 2, HALF], F32, name="gains")
+        swapped = keep.tile([P, 4, 2, HALF], F32, name="swapped")
+
+        def spread_gains():
+            ps = bank(3)
+            nc.tensor.matmul(ps[:], lhsT=ident[:, 0:1].to_broadcast([P, P]), rhs=rows_g[:], start=True, stop=True)
+            pv = ps[:].rearrange("p (j s d) -> p j s d", s=2, d=HALF)
+            nc.scalar.copy(out=gains[:], in_=pv)
+            nc.scalar.copy(out=swapped[:, :, 0, :], in_=pv[:, :, 1, :])
+            nc.scalar.copy(out=swapped[:, :, 1, :], in_=pv[:, :, 0, :])
+
+        table = {}
+
+        def build_tables(s):
+            for qk in range(2):
+                j = 2 * s + qk
+                t_cos = keep.tile([P, 4, 2, HALF], F32, name=f"tcos{j}")
+                t_sin = keep.tile([P, 4, 2, HALF], F32, name=f"tsin{j}")
+                shape = [P, 4, 2, HALF]
+                nc.vector.tensor_mul(t_cos[:], cos[:, 4 * s : 4 * s + 4, :].unsqueeze(2).to_broadcast(shape),
+                                     gains[:, j, :, :].unsqueeze(1).to_broadcast(shape))
+                nc.vector.tensor_mul(t_sin[:], sin[:, 4 * s : 4 * s + 4, :, :],
+                                     swapped[:, j, :, :].unsqueeze(1).to_broadcast(shape))
+                table[(s, qk)] = (t_cos, t_sin)
+
+        groups = [(s, b, n, m) for s in range(2) for b in range(B) for n in range(6) for m in range(4)]
+        w_of = {(0, n): n for n in range(6)}
+        w_of.update({(1, 0): 6, (1, 1): 7, (1, 2): 0, (1, 3): 1, (1, 4): 2, (1, 5): 3})
+        x_of = {(0, 0): 0, (0, 1): 1, (1, 0): 2, (1, 1): 0}
+        acc = {}
+
+        def one_pass(i, g):
+            s, b, n, m = groups[i]
+            if g == 0:
+                acc[i] = bank(i + 4)
+            xc, xs = x_slot[x_of[(s, b)]]
+            wc, ws = w_slot[w_of[(s, n)]]
+            nc.tensor.matmul_mx(
+                out=acc[i][:],
+                lhsT=xc[:, g, 256 * m : 256 * (m + 1)].bitcast(FP4X4), lhsT_scale=xs[:, g, P * m : P * (m + 1)],
+                rhs=wc[:, g, :].bitcast(FP4X4), rhs_scale=ws[:, g, :],
+                start=(g == 0), stop=(g == PASSES - 1))
+
+        z_of = {}
+
+        def step_cos(job):
+            s, b, qk, m, z, rstd = job
+            t1 = work.tile([P, H, DH], F32, name="t1", tag="t1", bufs=4)
+            tab = table[(s, qk)][0][:, m, :, :].rearrange("p s d -> p (s d)")
+            nc.vector.tensor_mul(t1[:], z[:], tab.unsqueeze(1).to_broadcast([P, H, DH]))
+            return t1
+
+        def step_sin(job):
+            s, b, qk, m, z, rstd = job
+            t2 = work.tile([P, H, DH], F32, name="t2", tag="t2", bufs=2)
+            halves = "p h (s d) -> p h s d"
+            tab = table[(s, qk)][1][:, m, :, :]
+            nc.vector.tensor_mul(t2[:].rearrange(halves, s=2), z[:].rearrange(halves, s=2)[:, :, ::-1, :],
+                                 tab.unsqueeze(1).to_broadcast([P, H, 2, HALF]))
+            return t2
+
+        def step_add(job, t1, t2):
+            s, b, qk, m, z, rstd = job
+            nc.vector.tensor_add(t1[:], t1[:], t2[:])
+            for h in range(H):
+                nc.scalar.activation(out=t1[:, h, :], in_=t1[:, h, :], func=ACT.Copy, scale=rstd[:, h : h + 1])
+            p0 = N1 * s + P * m
+            nc.sync.dma_start(out=outs[qk][b, :, p0 : p0 + P, :].rearrange("h p d -> p h d"), in_=t1[:])
+
+        pending = []
+
+        def advance():
+            if not pending:
+                return
+            entry = pending[0]
+            if len(entry) == 1:
+                entry.append(step_cos(entry[0]))
+            elif len(entry) == 2:
+                entry.append(step_sin(entry[0]))
+            else:
+                step_add(entry[0], entry[1], entry[2])
+                pending.remove(entry)
+
+        def epilogue(i):
+            s, b, n, m = groups[i]
+            which, half = n // 2, n % 2
+            if which == 2:
+                vo = work.tile([P, 4, DH], F32, name="vo", tag="vo", bufs=4)
+                nc.vector.tensor_add(vo[:].rearrange("p h d -> p (h d)"), acc[i][:], bias[n][:])
+                p0 = N1 * s + P * m
+                nc.sync.dma_start(out=outs[2][b, 4 * half : 4 * half + 4, p0 : p0 + P, :].rearrange("h p d -> p h d"), in_=vo[:])
+                return
+            if half == 0:
+                z = work.tile([P, H, DH], F32, name="z", tag="z", bufs=8)
+                ss = work.tile([P, H], F32, name="ss", tag="ss", bufs=8)
+                z_of[(which, m)] = (z, ss)
+            z, ss = z_of[(which, m)]
+            nc.vector.tensor_add(z[:, 4 * half : 4 * half + 4, :].rearrange("p h d -> p (h d)"), acc[i][:], bias[n][:])
+            for h in range(4 * half, 4 * half + 4):
+                junk = work.tile([P, DH], BF16, name="junk", tag="junk", bufs=2)
+                nc.scalar.activation(out=junk[:], in_=z[:, h, :], func=ACT.Square, accum_out=ss[:, h : h + 1])
+            if half == 1:
+                rstd = work.tile([P, H], F32, name="rstd", tag="rstd", bufs=8)
+                nc.scalar.activation(out=rstd[:], in_=ss[:], func=ACT.Abs_reciprocal_sqrt, scale=1.0 / DH, bias=1e-6)
+                pending.append([(s, b, which, m, z, rstd)])
+
+        later_loads = {
+            28: lambda: load_block(w_slot[6], w_words[1], w_scales[1], 0),
+            30: lambda: load_block(w_slot[7], w_words[1], w_scales[1], 1),
+            32: lambda: load_block(x_slot[2], x_words[1], x_scales[1], 0),
+            34: lambda: load_block(w_slot[0], w_words[1], w_scales[1], 2),
+            36: lambda: load_block(x_slot[0], x_words[1], x_scales[1], 1),
+            38: lambda: load_block(w_slot[1], w_words[1], w_scales[1], 3),
+            42: lambda: load_block(w_slot[2], w_words[1], w_scales[1], 4),
+            46: lambda: load_block(w_slot[3], w_words[1], w_scales[1], 5),
+        }
+
+        for i in range(len(groups)):
+            s, b, n, m = groups[i]
+            if i == 0:
+                for g in range(PASSES):
+                    for k in range(4):
+                        one_pass(k, g)
+                    if g == 3:
+                        spread_gains()
+                build_tables(0)
+            elif i >= 4:
+                for g in range(PASSES):
+                    one_pass(i, g)
+            epilogue(i)
+            for r in range(2 if i >= 72 else 1):
+                advance()
+            if i == 20:
+                build_tables(1)
+            if i in later_loads:
+                later_loads[i]()
+            if s == 0 and b == 1 and m == 3:
+                nc.gpsimd.dma_start(out=bias[n][:], in_=b_qkv2[COLS * n : COLS * (n + 1)].partition_broadcast(P))
+        while pending:
+            advance()

@@ -19,6 +19,7 @@ PASSES = D // 512
 COLS = 512
 W_SLOTS = 8
 X_SLOTS = 3
+WARM = 6
 FLOPS = 2 * 2 * (B * N1) * D * (3 * H * DH)
 
 
@@ -75,17 +76,16 @@ def tile_mmattn_pa_kernel(
 
         rows_b = keep.tile([P, COLS], BF16, name="rows_b")
         rows_g = keep.tile([P, COLS], BF16, name="rows_g")
+        zeros = keep.tile([P, COLS], BF16, name="zeros")
         nc.vector.memset(rows_b[:].bitcast(I32), 0)
-        zero_plane(nc.gpsimd, w_slot[0])
+        nc.vector.memset(zeros[:].bitcast(I32), 0)
         zero_plane(nc.vector, x_slot[0])
+        zero_plane(nc.vector, w_slot[0])
         nc.vector.memset(rows_g[:].bitcast(I32), 0)
-        zero_plane(nc.vector, w_slot[1])
-        zero_plane(nc.vector, w_slot[2])
-        zero_plane(nc.vector, w_slot[3])
 
-        nc.gpsimd.dma_start(out=rows_b[0:6, :], in_=b_qkv1.rearrange("(r c) -> r c", c=COLS))
         ident = keep.tile([P, P], BF16, name="ident")
         make_identity(nc, ident[:])
+        nc.gpsimd.dma_start(out=rows_b[0:6, :], in_=b_qkv1.rearrange("(r c) -> r c", c=COLS))
         pos = keep.tile([P, 8], F32, name="pos")
         nc.gpsimd.iota(pos[:], [[P, 8]], base=0, channel_multiplier=1, allow_small_or_imprecise_dtypes=True)
         for j, gain in enumerate((qg1, kg1, qg2, kg2)):
@@ -102,16 +102,26 @@ def tile_mmattn_pa_kernel(
         for g0, g1 in ((1, 2), (2, 4), (4, 8)):
             load_codes(w_slot[0], w_words[0], 0, g0, g1)
             load_codes(x_slot[0], x_words[0], 0, g0, g1)
-        for n in (1, 2, 3, 4):
-            load_block(w_slot[n], w_words[0], w_scales[0], n)
-        load_block(w_slot[5], w_words[0], w_scales[0], 5)
-        load_block(x_slot[1], x_words[0], x_scales[0], 1)
+
+        idle = bank(3)
+        for k in range(WARM):
+            nc.tensor.matmul(idle[:], lhsT=zeros[:, 0:P], rhs=zeros[:], start=True, stop=True)
 
         bias = [keep.tile([P, COLS], BF16, name=f"bias{n}") for n in range(6)]
         for n in range(6):
             ps = bank(n % 4)
             nc.tensor.matmul(ps[:], lhsT=ident[:, n : n + 1].to_broadcast([P, P]), rhs=rows_b[:], start=True, stop=True)
-            nc.scalar.copy(out=bias[n][:], in_=ps[:])
+            if n % 2 == 0:
+                nc.scalar.copy(out=bias[n][:], in_=ps[:])
+            else:
+                nc.vector.tensor_copy(out=bias[n][:], in_=ps[:])
+
+        zero_plane(nc.vector, w_slot[1])
+        zero_plane(nc.vector, w_slot[2])
+        zero_plane(nc.vector, w_slot[3])
+        for n in (1, 2, 3, 4, 5):
+            load_block(w_slot[n], w_words[0], w_scales[0], n)
+        load_block(x_slot[1], x_words[0], x_scales[0], 1)
 
         turns = work.tile([P, 2, 8, HALF], F32, name="turns", tag="z", bufs=8)
         nc.vector.tensor_scalar_mul(turns[:, 0, :, 0:1], pos[:].unsqueeze(2), 1.0 / (2.0 * math.pi))
@@ -164,16 +174,16 @@ def tile_mmattn_pa_kernel(
         x_of = {(0, 0): 0, (0, 1): 1, (1, 0): 2, (1, 1): 0}
         acc = {}
 
-        def one_pass(i, g):
+        def one_pass(i, g, c0=0, c1=COLS):
             s, b, n, m = groups[i]
-            if g == 0:
+            if i not in acc:
                 acc[i] = bank(i + 4)
             xc, xs = x_slot[x_of[(s, b)]]
             wc, ws = w_slot[w_of[(s, n)]]
             nc.tensor.matmul_mx(
-                out=acc[i][:],
+                out=acc[i][:, c0:c1],
                 lhsT=xc[:, g, 256 * m : 256 * (m + 1)].bitcast(FP4X4), lhsT_scale=xs[:, g, P * m : P * (m + 1)],
-                rhs=wc[:, g, :].bitcast(FP4X4), rhs_scale=ws[:, g, :],
+                rhs=wc[:, g, 2 * c0 : 2 * c1].bitcast(FP4X4), rhs_scale=ws[:, g, c0:c1],
                 start=(g == 0), stop=(g == PASSES - 1))
 
         z_of = {}
@@ -216,14 +226,20 @@ def tile_mmattn_pa_kernel(
                 step_add(entry[0], entry[1], entry[2])
                 pending.remove(entry)
 
+        def value_epilogue(i, c0, c1):
+            s, b, n, m = groups[i]
+            h0, h1 = c0 // DH, c1 // DH
+            first = 4 * (n % 2)
+            vo = work.tile([P, 4, DH], F32, name="vo", tag="vo", bufs=4)
+            nc.vector.tensor_add(vo[:, h0:h1, :].rearrange("p h d -> p (h d)"), acc[i][:, c0:c1], bias[n][:, c0:c1])
+            p0 = N1 * s + P * m
+            nc.sync.dma_start(out=outs[2][b, first + h0 : first + h1, p0 : p0 + P, :].rearrange("h p d -> p h d"), in_=vo[:, h0:h1, :])
+
         def epilogue(i):
             s, b, n, m = groups[i]
             which, half = n // 2, n % 2
             if which == 2:
-                vo = work.tile([P, 4, DH], F32, name="vo", tag="vo", bufs=4)
-                nc.vector.tensor_add(vo[:].rearrange("p h d -> p (h d)"), acc[i][:], bias[n][:])
-                p0 = N1 * s + P * m
-                nc.sync.dma_start(out=outs[2][b, 4 * half : 4 * half + 4, p0 : p0 + P, :].rearrange("h p d -> p h d"), in_=vo[:])
+                value_epilogue(i, 0, COLS)
                 return
             if half == 0:
                 z = work.tile([P, H, DH], F32, name="z", tag="z", bufs=8)
@@ -256,17 +272,23 @@ def tile_mmattn_pa_kernel(
                 for g in range(PASSES):
                     for k in range(4):
                         one_pass(k, g)
-                    if g == 3:
+                    if g == 6:
                         spread_gains()
-                build_tables(0)
+            elif i == len(groups) - 1:
+                for c0 in (0, COLS // 2):
+                    acc[i] = bank(i + 4 + c0 // (COLS // 2))
+                    for g in range(PASSES):
+                        one_pass(i, g, c0, c0 + COLS // 2)
+                    value_epilogue(i, c0, c0 + COLS // 2)
+                continue
             elif i >= 4:
                 for g in range(PASSES):
                     one_pass(i, g)
             epilogue(i)
             for r in range(2 if i >= 72 else 1):
                 advance()
-            if i == 20:
-                build_tables(1)
+            if i in (3, 20):
+                build_tables(0 if i == 3 else 1)
             if i in later_loads:
                 later_loads[i]()
             if s == 0 and b == 1 and m == 3:

@@ -57,11 +57,11 @@ def tile_mmattn_pa_kernel(
                 out=slot[0][:, g0:g1, :].bitcast(I32),
                 in_=words[g0:g1, :, 2 * COLS * c : 2 * COLS * (c + 1)].rearrange("g p c -> p g c").bitcast(I32))
 
-        def load_scales(slot, scales, c):
+        def load_scales(slot, scales, c, g0=0, g1=PASSES):
             for q in range(4):
                 nc.sync.dma_start(
-                    out=slot[1][32 * q : 32 * q + 4, :, :].bitcast(I32),
-                    in_=scales[:, 4 * q : 4 * q + 4, COLS * c : COLS * (c + 1)].rearrange("g r n -> r g n").bitcast(I32))
+                    out=slot[1][32 * q : 32 * q + 4, g0:g1, :].bitcast(I32),
+                    in_=scales[g0:g1, 4 * q : 4 * q + 4, COLS * c : COLS * (c + 1)].rearrange("g r n -> r g n").bitcast(I32))
 
         def load_block(slot, words, scales, c):
             load_scales(slot, scales, c)
@@ -97,11 +97,15 @@ def tile_mmattn_pa_kernel(
         zero_plane(nc.gpsimd, w_slot[7])
         zero_plane(nc.gpsimd, x_slot[2])
 
-        load_scales(x_slot[0], x_scales[0], 0)
-        load_scales(w_slot[0], w_scales[0], 0)
-        for g0, g1 in ((1, 2), (2, 4), (4, 8)):
+        load_scales(x_slot[0], x_scales[0], 0, 0, 3)
+        load_scales(w_slot[0], w_scales[0], 0, 0, 3)
+        for g0, g1 in ((1, 2), (2, 4)):
             load_codes(w_slot[0], w_words[0], 0, g0, g1)
             load_codes(x_slot[0], x_words[0], 0, g0, g1)
+        load_scales(x_slot[0], x_scales[0], 0, 3, 8)
+        load_scales(w_slot[0], w_scales[0], 0, 3, 8)
+        load_codes(w_slot[0], w_words[0], 0, 4, 8)
+        load_codes(x_slot[0], x_words[0], 0, 4, 8)
 
         idle = bank(3)
         for k in range(WARM):
@@ -123,7 +127,7 @@ def tile_mmattn_pa_kernel(
             load_block(w_slot[n], w_words[0], w_scales[0], n)
         load_block(x_slot[1], x_words[0], x_scales[0], 1)
 
-        turns = work.tile([P, 2, 8, HALF], F32, name="turns", tag="z", bufs=8)
+        turns = work.tile([P, 2, 8, HALF], F32, name="turns", tag="z", bufs=7)
         nc.vector.tensor_scalar_mul(turns[:, 0, :, 0:1], pos[:].unsqueeze(2), 1.0 / (2.0 * math.pi))
         w = 1
         while w < HALF:
@@ -132,7 +136,7 @@ def tile_mmattn_pa_kernel(
         nc.vector.tensor_scalar_add(turns[:, 1, :, :], turns[:, 0, :, :], 0.25)
         whole_i = work.tile([P, 1024], I32, name="whole_i", tag="t1", bufs=4)
         whole_f = work.tile([P, 1024], F32, name="whole_f", tag="t2", bufs=2)
-        frac = work.tile([P, 2, 8, HALF], F32, name="frac", tag="z", bufs=8)
+        frac = work.tile([P, 2, 8, HALF], F32, name="frac", tag="z", bufs=7)
         flat_turns = turns[:].rearrange("p a t d -> p (a t d)")
         nc.vector.tensor_copy(out=whole_i[:], in_=flat_turns)
         nc.vector.tensor_copy(out=whole_f[:], in_=whole_i[:])
@@ -230,7 +234,7 @@ def tile_mmattn_pa_kernel(
             s, b, n, m = groups[i]
             h0, h1 = c0 // DH, c1 // DH
             first = 4 * (n % 2)
-            vo = work.tile([P, 4, DH], F32, name="vo", tag="vo", bufs=4)
+            vo = work.tile([P, 4, DH], F32, name="vo", tag="vo", bufs=6)
             nc.vector.tensor_add(vo[:, h0:h1, :].rearrange("p h d -> p (h d)"), acc[i][:, c0:c1], bias[n][:, c0:c1])
             p0 = N1 * s + P * m
             nc.sync.dma_start(out=outs[2][b, first + h0 : first + h1, p0 : p0 + P, :].rearrange("h p d -> p h d"), in_=vo[:, h0:h1, :])
@@ -242,7 +246,7 @@ def tile_mmattn_pa_kernel(
                 value_epilogue(i, 0, COLS)
                 return
             if half == 0:
-                z = work.tile([P, H, DH], F32, name="z", tag="z", bufs=8)
+                z = work.tile([P, H, DH], F32, name="z", tag="z", bufs=7)
                 ss = work.tile([P, H], F32, name="ss", tag="ss", bufs=8)
                 z_of[(which, m)] = (z, ss)
             z, ss = z_of[(which, m)]

@@ -97,13 +97,13 @@ def tile_mmattn_pa_kernel(
         zero_plane(nc.gpsimd, w_slot[7])
         zero_plane(nc.gpsimd, x_slot[2])
 
-        load_scales(x_slot[0], x_scales[0], 0, 0, 3)
-        load_scales(w_slot[0], w_scales[0], 0, 0, 3)
+        load_scales(x_slot[0], x_scales[0], 0, 0, 4)
+        load_scales(w_slot[0], w_scales[0], 0, 0, 4)
         for g0, g1 in ((1, 2), (2, 4)):
             load_codes(w_slot[0], w_words[0], 0, g0, g1)
             load_codes(x_slot[0], x_words[0], 0, g0, g1)
-        load_scales(x_slot[0], x_scales[0], 0, 3, 8)
-        load_scales(w_slot[0], w_scales[0], 0, 3, 8)
+        load_scales(x_slot[0], x_scales[0], 0, 4, 8)
+        load_scales(w_slot[0], w_scales[0], 0, 4, 8)
         load_codes(w_slot[0], w_words[0], 0, 4, 8)
         load_codes(x_slot[0], x_words[0], 0, 4, 8)
 
@@ -121,11 +121,9 @@ def tile_mmattn_pa_kernel(
                 nc.vector.tensor_copy(out=bias[n][:], in_=ps[:])
 
         zero_plane(nc.vector, w_slot[1])
-        zero_plane(nc.vector, w_slot[2])
-        zero_plane(nc.vector, w_slot[3])
-        for n in (1, 2, 3, 4, 5):
-            load_block(w_slot[n], w_words[0], w_scales[0], n)
-        load_block(x_slot[1], x_words[0], x_scales[0], 1)
+        load_scales(w_slot[1], w_scales[0], 1)
+        for g in range(0, PASSES, 2):
+            load_codes(w_slot[1], w_words[0], 1, g, g + 2)
 
         turns = work.tile([P, 2, 8, HALF], F32, name="turns", tag="z", bufs=7)
         nc.vector.tensor_scalar_mul(turns[:, 0, :, 0:1], pos[:].unsqueeze(2), 1.0 / (2.0 * math.pi))
@@ -141,11 +139,18 @@ def tile_mmattn_pa_kernel(
         nc.vector.tensor_copy(out=whole_i[:], in_=flat_turns)
         nc.vector.tensor_copy(out=whole_f[:], in_=whole_i[:])
         nc.vector.tensor_sub(frac[:].rearrange("p a t d -> p (a t d)"), flat_turns, whole_f[:])
+        zero_plane(nc.vector, w_slot[2])
+        zero_plane(nc.vector, w_slot[3])
+        for n in (2, 3, 4, 5):
+            load_block(w_slot[n], w_words[0], w_scales[0], n)
+        load_block(x_slot[1], x_words[0], x_scales[0], 1)
         cos = keep.tile([P, 8, HALF], F32, name="cos")
         sin = keep.tile([P, 8, 2, HALF], F32, name="sin")
-        nc.scalar.activation(out=cos[:], in_=frac[:, 1, :, :], func=ACT.Sin, scale=2.0 * math.pi)
-        nc.scalar.activation(out=sin[:, :, 0, :], in_=frac[:, 0, :, :], func=ACT.Sin, scale=-2.0 * math.pi)
-        nc.scalar.activation(out=sin[:, :, 1, :], in_=frac[:, 0, :, :], func=ACT.Sin, scale=2.0 * math.pi)
+
+        def rotation():
+            nc.scalar.activation(out=cos[:], in_=frac[:, 1, :, :], func=ACT.Sin, scale=2.0 * math.pi)
+            nc.scalar.activation(out=sin[:, :, 0, :], in_=frac[:, 0, :, :], func=ACT.Sin, scale=-2.0 * math.pi)
+            nc.scalar.activation(out=sin[:, :, 1, :], in_=frac[:, 0, :, :], func=ACT.Sin, scale=2.0 * math.pi)
 
         gains = keep.tile([P, 4, 2, HALF], F32, name="gains")
         swapped = keep.tile([P, 4, 2, HALF], F32, name="swapped")
@@ -272,12 +277,13 @@ def tile_mmattn_pa_kernel(
 
         for i in range(len(groups)):
             s, b, n, m = groups[i]
-            if i == 0:
+            if i in (0, 4, 8):
                 for g in range(PASSES):
-                    for k in range(4):
+                    for k in range(i, i + 4):
                         one_pass(k, g)
-                    if g == 6:
+                    if i == 0 and g == 6:
                         spread_gains()
+                        rotation()
             elif i == len(groups) - 1:
                 for c0 in (0, COLS // 2):
                     acc[i] = bank(i + 4 + c0 // (COLS // 2))
@@ -285,7 +291,7 @@ def tile_mmattn_pa_kernel(
                         one_pass(i, g, c0, c0 + COLS // 2)
                     value_epilogue(i, c0, c0 + COLS // 2)
                 continue
-            elif i >= 4:
+            elif i >= 12:
                 for g in range(PASSES):
                     one_pass(i, g)
             epilogue(i)

@@ -19,7 +19,7 @@ PASSES = D // 512
 COLS = 512
 W_SLOTS = 8
 X_SLOTS = 3
-WARM = 6
+WARM = 10
 FLOPS = 2 * 2 * (B * N1) * D * (3 * H * DH)
 
 
@@ -74,10 +74,8 @@ def tile_mmattn_pa_kernel(
         load_codes(w_slot[0], w_words[0], 0, 0, 1)
         load_codes(x_slot[0], x_words[0], 0, 0, 1)
 
-        rows_b = keep.tile([P, COLS], BF16, name="rows_b")
         rows_g = keep.tile([P, COLS], BF16, name="rows_g")
         zeros = keep.tile([P, COLS], BF16, name="zeros")
-        nc.vector.memset(rows_b[:].bitcast(I32), 0)
         nc.vector.memset(zeros[:].bitcast(I32), 0)
         zero_plane(nc.vector, x_slot[0])
         zero_plane(nc.vector, w_slot[0])
@@ -85,7 +83,6 @@ def tile_mmattn_pa_kernel(
 
         ident = keep.tile([P, P], BF16, name="ident")
         make_identity(nc, ident[:])
-        nc.gpsimd.dma_start(out=rows_b[0:6, :], in_=b_qkv1.rearrange("(r c) -> r c", c=COLS))
         pos = keep.tile([P, 8], F32, name="pos")
         nc.gpsimd.iota(pos[:], [[P, 8]], base=0, channel_multiplier=1, allow_small_or_imprecise_dtypes=True)
         for j, gain in enumerate((qg1, kg1, qg2, kg2)):
@@ -97,12 +94,11 @@ def tile_mmattn_pa_kernel(
         zero_plane(nc.gpsimd, w_slot[7])
         zero_plane(nc.gpsimd, x_slot[2])
 
-        load_scales(x_slot[0], x_scales[0], 0, 0, 4)
+        load_scales(x_slot[0], x_scales[0], 0)
         load_scales(w_slot[0], w_scales[0], 0, 0, 4)
         for g0, g1 in ((1, 2), (2, 4)):
             load_codes(w_slot[0], w_words[0], 0, g0, g1)
             load_codes(x_slot[0], x_words[0], 0, g0, g1)
-        load_scales(x_slot[0], x_scales[0], 0, 4, 8)
         load_scales(w_slot[0], w_scales[0], 0, 4, 8)
         load_codes(w_slot[0], w_words[0], 0, 4, 8)
         load_codes(x_slot[0], x_words[0], 0, 4, 8)
@@ -112,18 +108,16 @@ def tile_mmattn_pa_kernel(
             nc.tensor.matmul(idle[:], lhsT=zeros[:, 0:P], rhs=zeros[:], start=True, stop=True)
 
         bias = [keep.tile([P, COLS], BF16, name=f"bias{n}") for n in range(6)]
-        for n in range(6):
-            ps = bank(n % 4)
-            nc.tensor.matmul(ps[:], lhsT=ident[:, n : n + 1].to_broadcast([P, P]), rhs=rows_b[:], start=True, stop=True)
-            if n % 2 == 0:
-                nc.scalar.copy(out=bias[n][:], in_=ps[:])
-            else:
-                nc.vector.tensor_copy(out=bias[n][:], in_=ps[:])
+
+        def load_bias(queue, b_qkv, n):
+            queue.dma_start(out=bias[n][:], in_=b_qkv[COLS * n : COLS * (n + 1)].partition_broadcast(P))
 
         zero_plane(nc.vector, w_slot[1])
         load_scales(w_slot[1], w_scales[0], 1)
         for g in range(0, PASSES, 2):
             load_codes(w_slot[1], w_words[0], 1, g, g + 2)
+        load_bias(nc.sync, b_qkv1, 0)
+        load_bias(nc.sync, b_qkv1, 1)
 
         turns = work.tile([P, 2, 8, HALF], F32, name="turns", tag="z", bufs=7)
         nc.vector.tensor_scalar_mul(turns[:, 0, :, 0:1], pos[:].unsqueeze(2), 1.0 / (2.0 * math.pi))
@@ -143,6 +137,9 @@ def tile_mmattn_pa_kernel(
         zero_plane(nc.vector, w_slot[3])
         for n in (2, 3, 4, 5):
             load_block(w_slot[n], w_words[0], w_scales[0], n)
+            if n < 4:
+                load_bias(nc.sync, b_qkv1, 2 * n - 2)
+                load_bias(nc.sync, b_qkv1, 2 * n - 1)
         load_block(x_slot[1], x_words[0], x_scales[0], 1)
         cos = keep.tile([P, 8, HALF], F32, name="cos")
         sin = keep.tile([P, 8, 2, HALF], F32, name="sin")
@@ -302,6 +299,6 @@ def tile_mmattn_pa_kernel(
             if i in later_loads:
                 later_loads[i]()
             if s == 0 and b == 1 and m == 3:
-                nc.gpsimd.dma_start(out=bias[n][:], in_=b_qkv2[COLS * n : COLS * (n + 1)].partition_broadcast(P))
+                load_bias(nc.gpsimd, b_qkv2, n)
         while pending:
             advance()

import math
from contextlib import ExitStack

import concourse.mybir as mybir
from concourse.masks import make_identity

F32 = mybir.dt.float32
BF16 = mybir.dt.bfloat16
I32 = mybir.dt.int32
U8 = mybir.dt.uint8
FP4X4 = mybir.dt.float4_e2m1fn_x4
ACT = mybir.ActivationFunctionType
ALU = mybir.AluOpType

P = 128
B, N1, D, H, DH = 2, 512, 4096, 8, 128
HALF = DH // 2
PASSES = D // 512
COLS = 512
W_SLOTS = 8
X_SLOTS = 3
WARM = 10
FLOPS = 2 * 2 * (B * N1) * D * (3 * H * DH)


def tile_mmattn_pa_kernel(
    tc, x_1_words, x_1_scales, x_2_words, x_2_scales,
    w_qkv1_words, w_qkv1_scales, b_qkv1, w_qkv2_words, w_qkv2_scales, b_qkv2,
    qg1, kg1, qg2, kg2, out_0, out_1, out_2,
):
    nc = tc.nc
    x_words = (x_1_words, x_2_words)
    x_scales = (x_1_scales, x_2_scales)
    w_words = (w_qkv1_words, w_qkv2_words)
    w_scales = (w_qkv1_scales, w_qkv2_scales)
    outs = (out_0, out_1, out_2)

    with ExitStack() as ctx:
        keep = ctx.enter_context(tc.tile_pool(name="keep", bufs=1))
        work = ctx.enter_context(tc.tile_pool(name="work", bufs=2))
        psum = ctx.enter_context(tc.psum_pool(name="psum", bufs=1))
        ctx.enter_context(tc.manual_schedule())

        def block_tiles(kind, k):
            codes = keep.tile([P, PASSES, 2 * COLS], U8, name=f"{kind}c{k}", align_bytes=256)
            plane = keep.tile([P, PASSES, COLS], U8, name=f"{kind}s{k}", align_bytes=256)
            return codes, plane

        w_slot = [block_tiles("w", k) for k in range(W_SLOTS)]
        x_slot = [block_tiles("x", k) for k in range(X_SLOTS)]

        def zero_plane(engine, slot):
            engine.memset(slot[1][:].rearrange("p g c -> p (g c)").bitcast(I32), 0)

        def load_codes(slot, words, c, g0, g1):
            nc.sync.dma_start(
                out=slot[0][:, g0:g1, :].bitcast(I32),
                in_=words[g0:g1, :, 2 * COLS * c : 2 * COLS * (c + 1)].rearrange("g p c -> p g c").bitcast(I32))

        def load_scales(slot, scales, c, g0=0, g1=PASSES):
            for q in range(4):
                nc.sync.dma_start(
                    out=slot[1][32 * q : 32 * q + 4, g0:g1, :].bitcast(I32),
                    in_=scales[g0:g1, 4 * q : 4 * q + 4, COLS * c : COLS * (c + 1)].rearrange("g r n -> r g n").bitcast(I32))

        def load_block(slot, words, scales, c):
            load_scales(slot, scales, c)
            load_codes(slot, words, c, 0, 4)
            load_codes(slot, words, c, 4, 8)

        def bank(i, name="bank"):
            return psum.tile([P, COLS], F32, name=f"{name}{i % 8}", tag=f"bank{i % 8}")

        load_codes(w_slot[0], w_words[0], 0, 0, 1)
        load_codes(x_slot[0], x_words[0], 0, 0, 1)

        rows_g = keep.tile([P, COLS], BF16, name="rows_g")
        zeros = keep.tile([P, COLS], BF16, name="zeros")
        nc.vector.memset(zeros[:].bitcast(I32), 0)
        zero_plane(nc.vector, x_slot[0])
        zero_plane(nc.vector, w_slot[0])
        nc.vector.memset(rows_g[:].bitcast(I32), 0)

        ident = keep.tile([P, P], BF16, name="ident")
        make_identity(nc, ident[:])
        pos = keep.tile([P, 8], F32, name="pos")
        nc.gpsimd.iota(pos[:], [[P, 8]], base=0, channel_multiplier=1, allow_small_or_imprecise_dtypes=True)
        for j, gain in enumerate((qg1, kg1, qg2, kg2)):
            nc.gpsimd.dma_start(out=rows_g[0:1, DH * j : DH * (j + 1)], in_=gain.rearrange("(r c) -> r c", r=1))
        zero_plane(nc.gpsimd, w_slot[4])
        zero_plane(nc.gpsimd, w_slot[5])
        zero_plane(nc.gpsimd, x_slot[1])
        zero_plane(nc.gpsimd, w_slot[6])
        zero_plane(nc.gpsimd, w_slot[7])
        zero_plane(nc.gpsimd, x_slot[2])

        load_scales(x_slot[0], x_scales[0], 0)
        load_scales(w_slot[0], w_scales[0], 0, 0, 4)
        for g0, g1 in ((1, 2), (2, 4)):
            load_codes(w_slot[0], w_words[0], 0, g0, g1)
            load_codes(x_slot[0], x_words[0], 0, g0, g1)
        load_scales(w_slot[0], w_scales[0], 0, 4, 8)
        load_codes(w_slot[0], w_words[0], 0, 4, 8)
        load_codes(x_slot[0], x_words[0], 0, 4, 8)

        idle = bank(3)
        for k in range(WARM):
            nc.tensor.matmul(idle[:], lhsT=zeros[:, 0:P], rhs=zeros[:], start=True, stop=True)

        bias = [keep.tile([P, COLS], BF16, name=f"bias{n}") for n in range(6)]

        def load_bias(queue, b_qkv, n):
            queue.dma_start(out=bias[n][:], in_=b_qkv[COLS * n : COLS * (n + 1)].partition_broadcast(P))

        zero_plane(nc.vector, w_slot[1])
        load_scales(w_slot[1], w_scales[0], 1)
        for g in range(0, PASSES, 2):
            load_codes(w_slot[1], w_words[0], 1, g, g + 2)
        load_bias(nc.sync, b_qkv1, 0)
        load_bias(nc.sync, b_qkv1, 1)

        turns = work.tile([P, 2, 8, HALF], F32, name="turns", tag="z", bufs=7)
        nc.vector.tensor_scalar_mul(turns[:, 0, :, 0:1], pos[:].unsqueeze(2), 1.0 / (2.0 * math.pi))
        w = 1
        while w < HALF:
            nc.vector.tensor_scalar_mul(turns[:, 0, :, w : 2 * w], turns[:, 0, :, 0:w], 10000.0 ** (-w / HALF))
            w *= 2
        nc.vector.tensor_scalar_add(turns[:, 1, :, :], turns[:, 0, :, :], 0.25)
        whole_i = work.tile([P, 1024], I32, name="whole_i", tag="t1", bufs=4)
        whole_f = work.tile([P, 1024], F32, name="whole_f", tag="t2", bufs=2)
        frac = work.tile([P, 2, 8, HALF], F32, name="frac", tag="z", bufs=7)
        flat_turns = turns[:].rearrange("p a t d -> p (a t d)")
        nc.vector.tensor_copy(out=whole_i[:], in_=flat_turns)
        nc.vector.tensor_copy(out=whole_f[:], in_=whole_i[:])
        nc.vector.tensor_sub(frac[:].rearrange("p a t d -> p (a t d)"), flat_turns, whole_f[:])
        zero_plane(nc.vector, w_slot[2])
        zero_plane(nc.vector, w_slot[3])
        for n in (2, 3, 4, 5):
            load_block(w_slot[n], w_words[0], w_scales[0], n)
            if n < 4:
                load_bias(nc.sync, b_qkv1, 2 * n - 2)
                load_bias(nc.sync, b_qkv1, 2 * n - 1)
        load_block(x_slot[1], x_words[0], x_scales[0], 1)
        cos = keep.tile([P, 8, HALF], F32, name="cos")
        sin = keep.tile([P, 8, 2, HALF], F32, name="sin")

        def rotation():
            nc.scalar.activation(out=cos[:], in_=frac[:, 1, :, :], func=ACT.Sin, scale=2.0 * math.pi)
            nc.scalar.activation(out=sin[:, :, 0, :], in_=frac[:, 0, :, :], func=ACT.Sin, scale=-2.0 * math.pi)
            nc.scalar.activation(out=sin[:, :, 1, :], in_=frac[:, 0, :, :], func=ACT.Sin, scale=2.0 * math.pi)

        gains = keep.tile([P, 4, 2, HALF], F32, name="gains")
        swapped = keep.tile([P, 4, 2, HALF], F32, name="swapped")

        def spread_gains():
            ps = bank(3)
            nc.tensor.matmul(ps[:], lhsT=ident[:, 0:1].to_broadcast([P, P]), rhs=rows_g[:], start=True, stop=True)
            pv = ps[:].rearrange("p (j s d) -> p j s d", s=2, d=HALF)
            nc.scalar.copy(out=gains[:], in_=pv)
            nc.scalar.copy(out=swapped[:, :, 0, :], in_=pv[:, :, 1, :])
            nc.scalar.copy(out=swapped[:, :, 1, :], in_=pv[:, :, 0, :])

        table = {}

        def build_tables(s):
            for qk in range(2):
                j = 2 * s + qk
                t_cos = keep.tile([P, 4, 2, HALF], F32, name=f"tcos{j}")
                t_sin = keep.tile([P, 4, 2, HALF], F32, name=f"tsin{j}")
                shape = [P, 4, 2, HALF]
                nc.vector.tensor_mul(t_cos[:], cos[:, 4 * s : 4 * s + 4, :].unsqueeze(2).to_broadcast(shape),
                                     gains[:, j, :, :].unsqueeze(1).to_broadcast(shape))
                nc.vector.tensor_mul(t_sin[:], sin[:, 4 * s : 4 * s + 4, :, :],
                                     swapped[:, j, :, :].unsqueeze(1).to_broadcast(shape))
                table[(s, qk)] = (t_cos, t_sin)

        groups = [(s, b, n, m) for s in range(2) for b in range(B) for n in range(6) for m in range(4)]
        w_of = {(0, n): n for n in range(6)}
        w_of.update({(1, 0): 6, (1, 1): 7, (1, 2): 0, (1, 3): 1, (1, 4): 2, (1, 5): 3})
        x_of = {(0, 0): 0, (0, 1): 1, (1, 0): 2, (1, 1): 0}
        acc = {}

        def one_pass(i, g, c0=0, c1=COLS):
            s, b, n, m = groups[i]
            if i not in acc:
                acc[i] = bank(i + 4)
            xc, xs = x_slot[x_of[(s, b)]]
            wc, ws = w_slot[w_of[(s, n)]]
            nc.tensor.matmul_mx(
                out=acc[i][:, c0:c1],
                lhsT=xc[:, g, 256 * m : 256 * (m + 1)].bitcast(FP4X4), lhsT_scale=xs[:, g, P * m : P * (m + 1)],
                rhs=wc[:, g, 2 * c0 : 2 * c1].bitcast(FP4X4), rhs_scale=ws[:, g, c0:c1],
                start=(g == 0), stop=(g == PASSES - 1))

        z_of = {}

        def step_cos(job):
            s, b, qk, m, z, rstd = job
            t1 = work.tile([P, H, DH], F32, name="t1", tag="t1", bufs=4)
            tab = table[(s, qk)][0][:, m, :, :].rearrange("p s d -> p (s d)")
            nc.vector.tensor_mul(t1[:], z[:], tab.unsqueeze(1).to_broadcast([P, H, DH]))
            return t1

        def step_sin(job):
            s, b, qk, m, z, rstd = job
            t2 = work.tile([P, H, DH], F32, name="t2", tag="t2", bufs=2)
            halves = "p h (s d) -> p h s d"
            tab = table[(s, qk)][1][:, m, :, :]
            nc.vector.tensor_mul(t2[:].rearrange(halves, s=2), z[:].rearrange(halves, s=2)[:, :, ::-1, :],
                                 tab.unsqueeze(1).to_broadcast([P, H, 2, HALF]))
            return t2

        def step_add(job, t1, t2):
            s, b, qk, m, z, rstd = job
            nc.vector.tensor_add(t1[:], t1[:], t2[:])
            for h in range(H):
                nc.scalar.activation(out=t1[:, h, :], in_=t1[:, h, :], func=ACT.Copy, scale=rstd[:, h : h + 1])
            p0 = N1 * s + P * m
            nc.sync.dma_start(out=outs[qk][b, :, p0 : p0 + P, :].rearrange("h p d -> p h d"), in_=t1[:])

        pending = []

        def advance():
            if not pending:
                return
            entry = pending[0]
            if len(entry) == 1:
                entry.append(step_cos(entry[0]))
            elif len(entry) == 2:
                entry.append(step_sin(entry[0]))
            else:
                step_add(entry[0], entry[1], entry[2])
                pending.remove(entry)

        def value_epilogue(i, c0, c1):
            s, b, n, m = groups[i]
            h0, h1 = c0 // DH, c1 // DH
            first = 4 * (n % 2)
            vo = work.tile([P, 4, DH], F32, name="vo", tag="vo", bufs=6)
            nc.vector.tensor_add(vo[:, h0:h1, :].rearrange("p h d -> p (h d)"), acc[i][:, c0:c1], bias[n][:, c0:c1])
            p0 = N1 * s + P * m
            nc.sync.dma_start(out=outs[2][b, first + h0 : first + h1, p0 : p0 + P, :].rearrange("h p d -> p h d"), in_=vo[:, h0:h1, :])

        def epilogue(i):
            s, b, n, m = groups[i]
            which, half = n // 2, n % 2
            if which == 2:
                value_epilogue(i, 0, COLS)
                return
            if half == 0:
                z = work.tile([P, H, DH], F32, name="z", tag="z", bufs=7)
                ss = work.tile([P, H], F32, name="ss", tag="ss", bufs=8)
                z_of[(which, m)] = (z, ss)
            z, ss = z_of[(which, m)]
            nc.vector.tensor_add(z[:, 4 * half : 4 * half + 4, :].rearrange("p h d -> p (h d)"), acc[i][:], bias[n][:])
            for h in range(4 * half, 4 * half + 4):
                junk = work.tile([P, DH], BF16, name="junk", tag="junk", bufs=2)
                nc.scalar.activation(out=junk[:], in_=z[:, h, :], func=ACT.Square, accum_out=ss[:, h : h + 1])
            if half == 1:
                rstd = work.tile([P, H], F32, name="rstd", tag="rstd", bufs=8)
                nc.scalar.activation(out=rstd[:], in_=ss[:], func=ACT.Abs_reciprocal_sqrt, scale=1.0 / DH, bias=1e-6)
                pending.append([(s, b, which, m, z, rstd)])

        later_loads = {
            28: lambda: load_block(w_slot[6], w_words[1], w_scales[1], 0),
            30: lambda: load_block(w_slot[7], w_words[1], w_scales[1], 1),
            32: lambda: load_block(x_slot[2], x_words[1], x_scales[1], 0),
            34: lambda: load_block(w_slot[0], w_words[1], w_scales[1], 2),
            36: lambda: load_block(x_slot[0], x_words[1], x_scales[1], 1),
            38: lambda: load_block(w_slot[1], w_words[1], w_scales[1], 3),
            42: lambda: load_block(w_slot[2], w_words[1], w_scales[1], 4),
            46: lambda: load_block(w_slot[3], w_words[1], w_scales[1], 5),
        }

        for i in range(len(groups)):
            s, b, n, m = groups[i]
            if i in (0, 4, 8):
                for g in range(PASSES):
                    for k in range(i, i + 4):
                        one_pass(k, g)
                    if i == 0 and g == 6:
                        spread_gains()
                        rotation()
            elif i == len(groups) - 1:
                for c0 in (0, COLS // 2):
                    acc[i] = bank(i + 4 + c0 // (COLS // 2))
                    for g in range(PASSES):
                        one_pass(i, g, c0, c0 + COLS // 2)
                    value_epilogue(i, c0, c0 + COLS // 2)
                continue
            elif i >= 12:
                for g in range(PASSES):
                    one_pass(i, g)
            epilogue(i)
            for r in range(2 if i >= 72 else 1):
                advance()
            if i in (3, 20):
                build_tables(0 if i == 3 else 1)
            if i in later_loads:
                later_loads[i]()
            if s == 0 and b == 1 and m == 3:
                load_bias(nc.gpsimd, b_qkv2, n)
        while pending:
            advance()
